import numpy as np
import ml_dtypes


BF16 = ml_dtypes.bfloat16


def bf(x):
    return np.asarray(x, np.float32).astype(BF16)


def f64(x):
    return np.asarray(x).astype(np.float64)


E2M1 = np.array([0.0, 0.5, 1.0, 1.5, 2.0, 3.0, 4.0, 6.0, -0.0, -0.5, -1.0, -1.5, -2.0, -3.0, -4.0, -6.0])


def pack_weight(w, fmt):
    k, n = w.shape
    w = f64(bf(w)).reshape(k // 32, 32, n)
    amax = np.abs(w).max(1)
    if fmt == "e4m3":
        byte = np.frexp(amax)[1] - 1 + 127 - 7
    else:
        mant, ex = np.frexp(amax / 6.0)
        byte = np.where(mant > 0.5, ex, ex - 1) + 127
    byte = np.clip(np.where(amax > 0, byte, 1), 1, 254)
    scaled = (w * np.exp2(127.0 - byte)[:, None, :]).reshape(k, n).astype(np.float32)
    by_word = np.ascontiguousarray(scaled.reshape(k // 512, 128, 4, n).transpose(0, 1, 3, 2))
    if fmt == "e4m3":
        words = by_word.astype(ml_dtypes.float8_e4m3fn).view(np.uint8)
    else:
        c = by_word.astype(ml_dtypes.float4_e2m1fn).view(np.uint8) & 0xF
        words = c[..., 0::2] | (c[..., 1::2] << 4)
    return np.ascontiguousarray(words), np.ascontiguousarray(byte.astype(np.uint8).reshape(k // 512, 16, n))


def unpack_weight(words, scales, fmt):
    g, p, n, _ = words.shape
    if fmt == "e4m3":
        vals = np.ascontiguousarray(words).view(ml_dtypes.float8_e4m3fn).astype(np.float64)
    else:
        nib = np.empty((g, p, n, 4), np.uint8)
        nib[..., 0::2] = words & 0xF
        nib[..., 1::2] = words >> 4
        vals = E2M1[nib]
    vals = vals * np.repeat(np.exp2(scales.astype(np.float64) - 127.0), 8, axis=1)[..., None]
    return vals.transpose(0, 1, 3, 2).reshape(g * 512, n)

def pack4(w):
    words, scales = pack_weight(w, "e2m1")
    return words.reshape(words.shape[0], 128, -1), scales


def unpack4(words, scales):
    return unpack_weight(words.reshape(words.shape[0], 128, -1, 2), scales, "e2m1")


def kspread(k):
    return np.exp2(np.repeat(np.random.randint(-6, 7, k // 32), 32).astype(np.float64))


B, T, C, D = 2, 512, 8192, 128
ROPE_BASE = 10000.0


def rotate_half(u):
    u1, u2 = np.split(u, 2, axis=-1)
    return np.concatenate([-u2, u1], axis=-1)


def rope_tables():
    inv_freq = 1.0 / (ROPE_BASE ** (f64(np.arange(0, D, 2)) / D))
    freqs = f64(np.arange(T))[:, None] * inv_freq[None, :]
    emb = np.concatenate([freqs, freqs], -1)
    return np.cos(emb), np.sin(emb)


def l2norm(u):
    return u / np.sqrt((u * u).sum(-1, keepdims=True))


def setup_inputs():
    s = kspread(C)
    x = np.random.standard_normal((B, T, C)) * s
    x_words, x_scales = pack4(np.ascontiguousarray(x.reshape(B * T, C).T))
    w = np.random.standard_normal((3 * D, C)) / np.sqrt(C) / s
    words, scales = pack4(np.ascontiguousarray(w.T))
    sqk = bf(0.75 * (1.0 + 0.25 * np.random.standard_normal(D)))
    return {"x_words": x_words,
            "x_scales": x_scales,
            "W_qkv_words": words,
            "W_qkv_scales": scales,
            "sqk": sqk}


def reference(x_words, x_scales, W_qkv_words, W_qkv_scales, sqk):
    xq = unpack4(x_words, x_scales).T.reshape(B, T, C)
    qkv = xq @ unpack4(W_qkv_words, W_qkv_scales)
    q, k, v = np.split(qkv, 3, axis=-1)
    cos, sin = rope_tables()
    q = q * cos + rotate_half(q) * sin
    k = k * cos + rotate_half(k) * sin
    g = f64(sqk)
    q = l2norm(q) * g
    k = l2norm(k) * g
    return q, k, v

@@ -1,0 +1,308 @@
+from contextlib import ExitStack
+import math
+
+import concourse.mybir as mybir
+
+FLOPS = 2 * 1024 * 8192 * 384
+
+F32 = mybir.dt.float32
+BF16 = mybir.dt.bfloat16
+I32 = mybir.dt.int32
+U8 = mybir.dt.uint8
+FP4X4 = mybir.dt.float4_e2m1fn_x4
+ALU = mybir.AluOpType
+ACTF = mybir.ActivationFunctionType
+
+P = 128
+PASSES = 16
+D = 128
+HALF = 64
+ROPE_BASE = 10000.0
+
+CODE_CHUNKS_A = [(0, 1), (1, 2), (2, 4), (4, 6), (6, 8), (8, 10), (10, 12), (12, 14), (14, 16)]
+SCALE_CHUNKS_A = [(0, 8), (8, 16)]
+SCALE_CHUNKS_W = [(0, 16)]
+CODE_CHUNKS_B = [(0, 2), (2, 4), (4, 6), (6, 8), (8, 10), (10, 12), (12, 14), (14, 16)]
+SCALE_CHUNKS_B = [(0, 8), (8, 16)]
+
+TWO_PI = 2.0 * math.pi
+C1 = 6.28125
+C2 = TWO_PI - C1
+WARM_MATMULS = 15
+SPLIT = 12
+
+
+def tile_attentionhead_pa_kernel(tc, x_words, x_scales, W_qkv_words, W_qkv_scales, sqk, out_0, out_1, out_2):
+    nc = tc.nc
+    q_out = out_0.rearrange("b t d -> (b t) d")
+    k_out = out_1.rearrange("b t d -> (b t) d")
+    v_out = out_2.rearrange("b t d -> (b t) d")
+
+    with ExitStack() as ctx:
+        keep = ctx.enter_context(tc.tile_pool(name="keep", bufs=1))
+        work = ctx.enter_context(tc.tile_pool(name="work", bufs=4))
+        psum = ctx.enter_context(tc.psum_pool(name="psum", bufs=1))
+        ctx.enter_context(tc.manual_schedule())
+
+        x_codes = [{}, {}]
+        x_planes = [{}, {}]
+        w_codes = {}
+        w_planes = {}
+        code_tiles = []
+        plane_tiles = []
+        for half, chunks in ((0, CODE_CHUNKS_A), (1, CODE_CHUNKS_B)):
+            for g0, g1 in chunks:
+                t = keep.tile([P, g1 - g0, 1024], U8, name="xc%d_%d" % (half, g0), align_bytes=64)
+                code_tiles.append(("x", half, g0, g1, t))
+                for g in range(g0, g1):
+                    x_codes[half][g] = (t, g - g0)
+        for g0, g1 in CODE_CHUNKS_A:
+            t = keep.tile([P, g1 - g0, 768], U8, name="wc_%d" % g0, align_bytes=64)
+            code_tiles.append(("w", 0, g0, g1, t))
+            for g in range(g0, g1):
+                w_codes[g] = (t, g - g0)
+        for half, chunks in ((0, SCALE_CHUNKS_A), (1, SCALE_CHUNKS_B)):
+            for g0, g1 in chunks:
+                t = keep.tile([P, g1 - g0, 512], U8, name="xs%d_%d" % (half, g0), align_bytes=64)
+                plane_tiles.append(("x", half, g0, g1, t))
+                for g in range(g0, g1):
+                    x_planes[half][g] = (t, g - g0)
+        for g0, g1 in SCALE_CHUNKS_W:
+            t = keep.tile([P, g1 - g0, 384], U8, name="ws_%d" % g0, align_bytes=64)
+            plane_tiles.append(("w", 0, g0, g1, t))
+            for g in range(g0, g1):
+                w_planes[g] = (t, g - g0)
+
+        def find(tiles, kind, half, g0):
+            for k, h, a, b, t in tiles:
+                if k == kind and h == half and a == g0:
+                    return a, b, t
+            raise ValueError("no such tile")
+
+        zero1 = keep.tile([P, 1], F32, name="zero1")
+        junk1 = keep.tile([P, 1], F32, name="junk1")
+        g_row = keep.tile([P, D], BF16, name="g_row")
+        ones = keep.tile([P, 512], BF16, name="ones")
+        gain = keep.tile([P, D], F32, name="gain")
+        pos_i = keep.tile([P, 4], I32, name="pos_i")
+        pos_f = keep.tile([P, 4], F32, name="pos_f")
+        freq = keep.tile([P, HALF], F32, name="freq")
+        ang = keep.tile([P, 256], F32, name="ang")
+        turns = keep.tile([P, 256], I32, name="turns")
+        red1 = keep.tile([P, 256], F32, name="red1")
+        red = keep.tile([P, 256], F32, name="red")
+        s2 = keep.tile([P, 256], F32, name="s2")
+        s4 = keep.tile([P, 256], F32, name="s4")
+        q2 = keep.tile([P, 256], F32, name="q2")
+        q4 = keep.tile([P, 256], F32, name="q4")
+        c2 = keep.tile([P, 256], F32, name="c2")
+        cos1 = keep.tile([P, 256], F32, name="cos1")
+        sin1 = keep.tile([P, 256], F32, name="sin1")
+        cos_t = keep.tile([P, 1024], F32, name="cos_t")
+        sin_t = keep.tile([P, 1024], F32, name="sin_t")
+
+        def zero_plane_vector(t):
+            nc.vector.memset(t[:].bitcast(I32), 0)
+
+        def zero_plane_gpsimd(t):
+            nc.gpsimd.memset(t[:].bitcast(F32), 0.0)
+
+        zero_plane_vector(find(plane_tiles, "x", 0, 0)[2])
+        zero_plane_vector(find(plane_tiles, "w", 0, 0)[2])
+        zero_plane_vector(find(plane_tiles, "x", 0, 8)[2])
+        nc.gpsimd.memset(ones[:], 1.0)
+        nc.gpsimd.memset(zero1[:], 0.0)
+        nc.gpsimd.memset(g_row[:], 0.0)
+        nc.gpsimd.dma_start(out=g_row[0:1, :], in_=sqk.rearrange("(o d) -> o d", o=1))
+        nc.gpsimd.iota(pos_i[:], pattern=[[P, 4]], base=0, channel_multiplier=1)
+        zero_plane_gpsimd(find(plane_tiles, "x", 1, 0)[2])
+        zero_plane_gpsimd(find(plane_tiles, "x", 1, 8)[2])
+
+        def load_codes(kind, half, g0):
+            a, b, t = find(code_tiles, kind, half, g0)
+            if kind == "x":
+                src = x_words[a:b, :, 1024 * half : 1024 * half + 1024]
+            else:
+                src = W_qkv_words[a:b, :, :]
+            nc.sync.dma_start(out=t[:].bitcast(I32), in_=src.rearrange("g p b -> p g b").bitcast(I32))
+
+        def load_planes(kind, half, g0):
+            a, b, t = find(plane_tiles, kind, half, g0)
+            for r in range(4):
+                if kind == "x":
+                    src = x_scales[a:b, r:16:4, 512 * half : 512 * half + 512]
+                else:
+                    src = W_qkv_scales[a:b, r:16:4, :]
+                nc.sync.dma_start(out=t[r:P:32, :, :].bitcast(I32), in_=src.rearrange("g q c -> q g c").bitcast(I32))
+
+        load_codes("x", 0, 0)
+        load_codes("w", 0, 0)
+        load_planes("x", 0, 0)
+        load_planes("w", 0, 0)
+        for g0 in (1, 2, 4, 6):
+            load_codes("x", 0, g0)
+            load_codes("w", 0, g0)
+        load_planes("x", 0, 8)
+        for g0 in (8, 10, 12, 14):
+            load_codes("x", 0, g0)
+            load_codes("w", 0, g0)
+        load_planes("x", 1, 0)
+        for g0 in (0, 2, 4, 6):
+            load_codes("x", 1, g0)
+        load_planes("x", 1, 8)
+        for g0 in (8, 10, 12, 14):
+            load_codes("x", 1, g0)
+
+        nc.scalar.activation(out=junk1[:], in_=zero1[:], func=ACTF.Sin)
+        g_ps = psum.tile([P, 512], F32, name="bank7")
+        for n in range(WARM_MATMULS):
+            nc.tensor.matmul(out=g_ps[:], lhsT=ones[:, 0:P], rhs=ones[:], start=True, stop=True)
+        nc.tensor.matmul(out=g_ps[:, 0:D], lhsT=ones[:, 0:P], rhs=g_row[:], start=True, stop=True)
+        nc.scalar.copy(out=gain[:], in_=g_ps[:, 0:D])
+
+        nc.vector.memset(freq[:, 0:1], 1.0)
+        w = 1
+        while w < HALF:
+            nc.vector.tensor_scalar(out=freq[:, w : 2 * w], in0=freq[:, 0:w], scalar1=ROPE_BASE ** (-w / 64.0), scalar2=None, op0=ALU.mult)
+            w *= 2
+        nc.vector.tensor_copy(out=pos_f[:], in_=pos_i[:])
+        for t in range(4):
+            nc.vector.tensor_scalar(out=ang[:, HALF * t : HALF * (t + 1)], in0=freq[:], scalar1=pos_f[:, t : t + 1], scalar2=None, op0=ALU.mult)
+        nc.vector.tensor_scalar(out=turns[:], in0=ang[:], scalar1=1.0 / TWO_PI, scalar2=0.25, op0=ALU.mult, op1=ALU.add)
+        nc.vector.scalar_tensor_tensor(out=red1[:], in0=turns[:], scalar=-C1, in1=ang[:], op0=ALU.mult, op1=ALU.add)
+        nc.vector.scalar_tensor_tensor(out=red[:], in0=turns[:], scalar=-C2, in1=red1[:], op0=ALU.mult, op1=ALU.add)
+        nc.scalar.activation(out=s4[:], in_=red[:], func=ACTF.Sin, scale=0.25)
+        nc.scalar.activation(out=s2[:], in_=red[:], func=ACTF.Sin, scale=0.5)
+        nc.scalar.activation(out=q4[:], in_=s4[:], func=ACTF.Square)
+        nc.scalar.activation(out=q2[:], in_=s2[:], func=ACTF.Square)
+        nc.vector.tensor_scalar(out=c2[:], in0=q4[:], scalar1=-2.0, scalar2=1.0, op0=ALU.mult, op1=ALU.add)
+        cos_v = cos_t[:].rearrange("p (t a h j) -> p t a h j", t=4, a=2, h=2)
+        sin_v = sin_t[:].rearrange("p (t a h j) -> p t a h j", t=4, a=2, h=2)
+        nc.scalar.activation(out=junk1[:], in_=freq[:, 0:1], func=ACTF.Sqrt)
+        nc.vector.tensor_scalar(out=cos1[:], in0=q2[:], scalar1=-2.0, scalar2=1.0, op0=ALU.mult, op1=ALU.add)
+        nc.vector.scalar_tensor_tensor(out=sin1[:], in0=s2[:], scalar=2.0, in1=c2[:], op0=ALU.mult, op1=ALU.mult)
+        for t in range(4):
+            for h in range(2):
+                nc.vector.tensor_tensor(out=cos_v[:, t, 0, h, :], in0=cos1[:, HALF * t : HALF * (t + 1)], in1=gain[:, HALF * h : HALF * (h + 1)], op=ALU.mult)
+                nc.vector.scalar_tensor_tensor(out=sin_v[:, t, 0, h, :], in0=sin1[:, HALF * t : HALF * (t + 1)], scalar=(-1.0 if h == 0 else 1.0), in1=gain[:, HALF * h : HALF * (h + 1)], op0=ALU.mult, op1=ALU.mult)
+        nc.vector.tensor_copy(out=cos_v[:, :, 1, :, :], in_=cos_v[:, :, 0, :, :])
+        nc.vector.tensor_copy(out=sin_v[:, :, 1, :, :], in_=sin_v[:, :, 0, :, :])
+
+        def mm(bank, part, i, g):
+            half = i // 4
+            il = i % 4
+            xt, xl = x_codes[half][g]
+            st, sl = x_planes[half][g]
+            wt, wl = w_codes[g]
+            pt, pl = w_planes[g]
+            if part == "qk":
+                c0, c1 = 0, 256
+            else:
+                c0, c1 = 256, 384
+            nc.tensor.matmul_mx(
+                out=bank[:, 0 : c1 - c0],
+                lhsT=xt[:, xl, 256 * il : 256 * (il + 1)].bitcast(FP4X4),
+                lhsT_scale=st[:, sl, P * il : P * (il + 1)],
+                rhs=wt[:, wl, 2 * c0 : 2 * c1].bitcast(FP4X4),
+                rhs_scale=pt[:, pl, c0:c1],
+                start=(g == 0),
+                stop=(g == PASSES - 1),
+            )
+
+        def finish_v(bank, i):
+            vt = work.tile([P, D], F32, name="vt")
+            nc.scalar.copy(out=vt[:], in_=bank[:, 0:D])
+            nc.sync.dma_start(out=v_out[P * i : P * (i + 1), :], in_=vt[:])
+
+        state = {}
+
+        def norms(bank, i):
+            sq = work.tile([P, D], F32, name="sq")
+            ss = work.tile([P, 2], F32, name="ss")
+            nc.scalar.activation(out=sq[:], in_=bank[:, 0:D], func=ACTF.Square, accum_out=ss[:, 0:1])
+            sq_k = work.tile([P, D], F32, name="sq")
+            nc.scalar.activation(out=sq_k[:], in_=bank[:, D : 2 * D], func=ACTF.Square, accum_out=ss[:, 1:2])
+            nrm = work.tile([P, 2], F32, name="nrm")
+            nc.scalar.activation(out=nrm[:], in_=ss[:], func=ACTF.Sqrt)
+            state[i] = [nrm]
+
+        def rope(bank, i):
+            t = i % 4
+            nrm = state[i][0]
+            t1 = work.tile([P, 256], F32, name="t1")
+            nc.vector.tensor_tensor(out=t1[:], in0=bank[:, 0:256], in1=cos_t[:, 256 * t : 256 * (t + 1)], op=ALU.mult)
+            t2 = work.tile([P, 256], F32, name="t2")
+            raw_v = bank[:, 0:256].rearrange("p (a h j) -> p a h j", a=2, h=2)
+            t2_v = t2[:].rearrange("p (a h j) -> p a h j", a=2, h=2)
+            nc.vector.tensor_tensor(out=t2_v[:, :, 0, :], in0=raw_v[:, :, 1, :], in1=sin_v[:, t, :, 0, :], op=ALU.mult)
+            nc.vector.tensor_tensor(out=t2_v[:, :, 1, :], in0=raw_v[:, :, 0, :], in1=sin_v[:, t, :, 1, :], op=ALU.mult)
+            sm = work.tile([P, 256], F32, name="sm")
+            nc.vector.tensor_tensor(out=sm[:], in0=t1[:], in1=t2[:], op=ALU.add)
+            rn = work.tile([P, 2], F32, name="rn")
+            nc.vector.reciprocal(out=rn[:], in_=nrm[:])
+            state[i] = [sm, rn]
+
+        def scale_store(i):
+            sm, rn = state[i]
+            res = work.tile([P, 256], F32, name="res")
+            nc.scalar.activation(out=res[:, 0:D], in_=sm[:, 0:D], func=ACTF.Copy, scale=rn[:, 0:1])
+            nc.scalar.activation(out=res[:, D : 2 * D], in_=sm[:, D : 2 * D], func=ACTF.Copy, scale=rn[:, 1:2])
+            nc.sync.dma_start(out=q_out[P * i : P * (i + 1), :], in_=res[:, 0:D])
+            nc.sync.dma_start(out=k_out[P * i : P * (i + 1), :], in_=res[:, D : 2 * D])
+
+        def new_bank(b):
+            bank = psum.tile([P, 512], F32, name="bank%d" % b)
+            return bank
+
+        qk_bank = {}
+        v_bank = {}
+        for i in range(4):
+            qk_bank[i] = new_bank(i)
+            v_bank[i] = new_bank(4 + i)
+        for g in range(PASSES):
+            if g < PASSES - 1:
+                for i in range(4):
+                    mm(qk_bank[i], "qk", i, g)
+                    mm(v_bank[i], "v", i, g)
+            else:
+                for i in range(4):
+                    mm(v_bank[i], "v", i, g)
+                for i in range(4):
+                    mm(qk_bank[i], "qk", i, g)
+        for i in range(4):
+            finish_v(v_bank[i], i)
+        norms(qk_bank[0], 0)
+        for i in range(4):
+            if i < 3:
+                norms(qk_bank[i + 1], i + 1)
+            rope(qk_bank[i], i)
+            scale_store(i)
+
+        for i in range(4, 8):
+            qk_bank[i] = new_bank(i)
+        for g in range(SPLIT):
+            for i in range(4, 8):
+                mm(qk_bank[i], "qk", i, g)
+        for i in range(4, 8):
+            for g in range(SPLIT, PASSES):
+                mm(qk_bank[i], "qk", i, g)
+        for i in range(4, 8):
+            v_bank[i] = new_bank(i - 4)
+            for g in range(PASSES):
+                mm(v_bank[i], "v", i, g)
+        norms(qk_bank[4], 4)
+        norms(qk_bank[5], 5)
+        rope(qk_bank[4], 4)
+        scale_store(4)
+        norms(qk_bank[6], 6)
+        rope(qk_bank[5], 5)
+        scale_store(5)
+        norms(qk_bank[7], 7)
+        finish_v(v_bank[4], 4)
+        rope(qk_bank[6], 6)
+        scale_store(6)
+        finish_v(v_bank[5], 5)
+        rope(qk_bank[7], 7)
+        scale_store(7)
+        finish_v(v_bank[6], 6)
+        finish_v(v_bank[7], 7)

@@ -19,16 +19,45 @@ D = 128
 HALF = 64
 ROPE_BASE = 10000.0
 
-CODE_CHUNKS_A = [(0, 1), (1, 2), (2, 4), (4, 6), (6, 8), (8, 10), (10, 12), (12, 14), (14, 16)]
-SCALE_CHUNKS_A = [(0, 8), (8, 16)]
-SCALE_CHUNKS_W = [(0, 16)]
-CODE_CHUNKS_B = [(0, 2), (2, 4), (4, 6), (6, 8), (8, 10), (10, 12), (12, 14), (14, 16)]
-SCALE_CHUNKS_B = [(0, 8), (8, 16)]
+LOADS = [
+    ("xc", 0, 0, 1),
+    ("wc", 0, 0, 1),
+    ("xs", 0, 0, 8),
+    ("ws", 0, 0, 16),
+    ("xc", 0, 1, 2),
+    ("wc", 0, 1, 2),
+    ("xc", 0, 2, 4),
+    ("wc", 0, 2, 4),
+    ("xc", 0, 4, 6),
+    ("wc", 0, 4, 6),
+    ("xc", 0, 6, 8),
+    ("wc", 0, 6, 8),
+    ("xs", 0, 8, 16),
+    ("xc", 0, 8, 10),
+    ("wc", 0, 8, 10),
+    ("xc", 0, 10, 12),
+    ("wc", 0, 10, 12),
+    ("xc", 0, 12, 14),
+    ("wc", 0, 12, 14),
+    ("xc", 0, 14, 16),
+    ("wc", 0, 14, 16),
+    ("xs", 1, 0, 8),
+    ("xc", 1, 0, 2),
+    ("xc", 1, 2, 4),
+    ("xc", 1, 4, 6),
+    ("xc", 1, 6, 8),
+    ("xs", 1, 8, 16),
+    ("xc", 1, 8, 10),
+    ("xc", 1, 10, 12),
+    ("xc", 1, 12, 14),
+    ("xc", 1, 14, 16),
+]
+VECTOR_ZEROS = 3
 
 TWO_PI = 2.0 * math.pi
 C1 = 6.28125
 C2 = TWO_PI - C1
-WARM_MATMULS = 15
+WARM_MATMULS = 22
 SPLIT = 12
 
 
@@ -46,38 +75,28 @@ def tile_attentionhead_pa_kernel(tc, x_words, x_scales, W_qkv_words, W_qkv_scale
 
         x_codes = [{}, {}]
         x_planes = [{}, {}]
-        w_codes = {}
+        wq_codes = {}
+        wv_codes = {}
         w_planes = {}
-        code_tiles = []
-        plane_tiles = []
-        for half, chunks in ((0, CODE_CHUNKS_A), (1, CODE_CHUNKS_B)):
-            for g0, g1 in chunks:
-                t = keep.tile([P, g1 - g0, 1024], U8, name="xc%d_%d" % (half, g0), align_bytes=64)
-                code_tiles.append(("x", half, g0, g1, t))
-                for g in range(g0, g1):
+        widths = {"xc": 1024, "wc": 768, "wq": 512, "wv": 256, "xs": 512, "ws": 384}
+        loads = []
+        for kind, half, g0, g1 in LOADS:
+            t = keep.tile([P, g1 - g0, widths[kind]], U8, name="%s%d_%d" % (kind, half, g0), align_bytes=64)
+            loads.append((kind, half, g0, g1, t))
+            for g in range(g0, g1):
+                if kind == "xc":
                     x_codes[half][g] = (t, g - g0)
-        for g0, g1 in CODE_CHUNKS_A:
-            t = keep.tile([P, g1 - g0, 768], U8, name="wc_%d" % g0, align_bytes=64)
-            code_tiles.append(("w", 0, g0, g1, t))
-            for g in range(g0, g1):
-                w_codes[g] = (t, g - g0)
-        for half, chunks in ((0, SCALE_CHUNKS_A), (1, SCALE_CHUNKS_B)):
-            for g0, g1 in chunks:
-                t = keep.tile([P, g1 - g0, 512], U8, name="xs%d_%d" % (half, g0), align_bytes=64)
-                plane_tiles.append(("x", half, g0, g1, t))
-                for g in range(g0, g1):
+                elif kind == "xs":
                     x_planes[half][g] = (t, g - g0)
-        for g0, g1 in SCALE_CHUNKS_W:
-            t = keep.tile([P, g1 - g0, 384], U8, name="ws_%d" % g0, align_bytes=64)
-            plane_tiles.append(("w", 0, g0, g1, t))
-            for g in range(g0, g1):
-                w_planes[g] = (t, g - g0)
-
-        def find(tiles, kind, half, g0):
-            for k, h, a, b, t in tiles:
-                if k == kind and h == half and a == g0:
-                    return a, b, t
-            raise ValueError("no such tile")
+                elif kind == "ws":
+                    w_planes[g] = (t, g - g0)
+                elif kind == "wc":
+                    wq_codes[g] = (t, g - g0, 0)
+                    wv_codes[g] = (t, g - g0, 512)
+                elif kind == "wq":
+                    wq_codes[g] = (t, g - g0, 0)
+                else:
+                    wv_codes[g] = (t, g - g0, 0)
 
         zero1 = keep.tile([P, 1], F32, name="zero1")
         junk1 = keep.tile([P, 1], F32, name="junk1")
@@ -101,57 +120,35 @@ def tile_attentionhead_pa_kernel(tc, x_words, x_scales, W_qkv_words, W_qkv_scale
         cos_t = keep.tile([P, 1024], F32, name="cos_t")
         sin_t = keep.tile([P, 1024], F32, name="sin_t")
 
-        def zero_plane_vector(t):
+        planes = [entry[4] for entry in loads if entry[0] in ("xs", "ws")]
+        for t in planes[:VECTOR_ZEROS]:
             nc.vector.memset(t[:].bitcast(I32), 0)
-
-        def zero_plane_gpsimd(t):
-            nc.gpsimd.memset(t[:].bitcast(F32), 0.0)
-
-        zero_plane_vector(find(plane_tiles, "x", 0, 0)[2])
-        zero_plane_vector(find(plane_tiles, "w", 0, 0)[2])
-        zero_plane_vector(find(plane_tiles, "x", 0, 8)[2])
         nc.gpsimd.memset(ones[:], 1.0)
         nc.gpsimd.memset(zero1[:], 0.0)
         nc.gpsimd.memset(g_row[:], 0.0)
         nc.gpsimd.dma_start(out=g_row[0:1, :], in_=sqk.rearrange("(o d) -> o d", o=1))
         nc.gpsimd.iota(pos_i[:], pattern=[[P, 4]], base=0, channel_multiplier=1)
-        zero_plane_gpsimd(find(plane_tiles, "x", 1, 0)[2])
-        zero_plane_gpsimd(find(plane_tiles, "x", 1, 8)[2])
+        for t in planes[VECTOR_ZEROS:]:
+            nc.gpsimd.memset(t[:].bitcast(F32), 0.0)
 
-        def load_codes(kind, half, g0):
-            a, b, t = find(code_tiles, kind, half, g0)
-            if kind == "x":
-                src = x_words[a:b, :, 1024 * half : 1024 * half + 1024]
+        for kind, half, a, b, t in loads:
+            if kind in ("xs", "ws"):
+                for r in range(4):
+                    if kind == "xs":
+                        src = x_scales[a:b, r:16:4, 512 * half : 512 * half + 512]
+                    else:
+                        src = W_qkv_scales[a:b, r:16:4, :]
+                    nc.sync.dma_start(out=t[r:P:32, :, :].bitcast(I32), in_=src.rearrange("g q c -> q g c").bitcast(I32))
             else:
-                src = W_qkv_words[a:b, :, :]
-            nc.sync.dma_start(out=t[:].bitcast(I32), in_=src.rearrange("g p b -> p g b").bitcast(I32))
-
-        def load_planes(kind, half, g0):
-            a, b, t = find(plane_tiles, kind, half, g0)
-            for r in range(4):
-                if kind == "x":
-                    src = x_scales[a:b, r:16:4, 512 * half : 512 * half + 512]
+                if kind == "xc":
+                    src = x_words[a:b, :, 1024 * half : 1024 * half + 1024]
+                elif kind == "wc":
+                    src = W_qkv_words[a:b, :, :]
+                elif kind == "wq":
+                    src = W_qkv_words[a:b, :, 0:512]
                 else:
-                    src = W_qkv_scales[a:b, r:16:4, :]
-                nc.sync.dma_start(out=t[r:P:32, :, :].bitcast(I32), in_=src.rearrange("g q c -> q g c").bitcast(I32))
-
-        load_codes("x", 0, 0)
-        load_codes("w", 0, 0)
-        load_planes("x", 0, 0)
-        load_planes("w", 0, 0)
-        for g0 in (1, 2, 4, 6):
-            load_codes("x", 0, g0)
-            load_codes("w", 0, g0)
-        load_planes("x", 0, 8)
-        for g0 in (8, 10, 12, 14):
-            load_codes("x", 0, g0)
-            load_codes("w", 0, g0)
-        load_planes("x", 1, 0)
-        for g0 in (0, 2, 4, 6):
-            load_codes("x", 1, g0)
-        load_planes("x", 1, 8)
-        for g0 in (8, 10, 12, 14):
-            load_codes("x", 1, g0)
+                    src = W_qkv_words[a:b, :, 512:768]
+                nc.sync.dma_start(out=t[:].bitcast(I32), in_=src.rearrange("g p b -> p g b").bitcast(I32))
 
         nc.scalar.activation(out=junk1[:], in_=zero1[:], func=ACTF.Sin)
         g_ps = psum.tile([P, 512], F32, name="bank7")
@@ -193,17 +190,18 @@ def tile_attentionhead_pa_kernel(tc, x_words, x_scales, W_qkv_words, W_qkv_scale
             il = i % 4
             xt, xl = x_codes[half][g]
             st, sl = x_planes[half][g]
-            wt, wl = w_codes[g]
             pt, pl = w_planes[g]
             if part == "qk":
                 c0, c1 = 0, 256
+                wt, wl, wo = wq_codes[g]
             else:
                 c0, c1 = 256, 384
+                wt, wl, wo = wv_codes[g]
             nc.tensor.matmul_mx(
                 out=bank[:, 0 : c1 - c0],
                 lhsT=xt[:, xl, 256 * il : 256 * (il + 1)].bitcast(FP4X4),
                 lhsT_scale=st[:, sl, P * il : P * (il + 1)],
-                rhs=wt[:, wl, 2 * c0 : 2 * c1].bitcast(FP4X4),
+                rhs=wt[:, wl, wo : wo + 2 * (c1 - c0)].bitcast(FP4X4),
                 rhs_scale=pt[:, pl, c0:c1],
                 start=(g == 0),
                 stop=(g == PASSES - 1),

@@ -58,7 +58,7 @@ TWO_PI = 2.0 * math.pi
 C1 = 6.28125
 C2 = TWO_PI - C1
 WARM_MATMULS = 22
-SPLIT = 12
+SPLIT = 8
 
 
 def tile_attentionhead_pa_kernel(tc, x_words, x_scales, W_qkv_words, W_qkv_scales, sqk, out_0, out_1, out_2):

@@ -257,16 +257,16 @@ def tile_attentionhead_pa_kernel(tc, x_words, x_scales, W_qkv_words, W_qkv_scale
         for i in range(4):
             qk_bank[i] = new_bank(i)
             v_bank[i] = new_bank(4 + i)
-        for g in range(PASSES):
-            if g < PASSES - 1:
-                for i in range(4):
-                    mm(qk_bank[i], "qk", i, g)
-                    mm(v_bank[i], "v", i, g)
-            else:
-                for i in range(4):
-                    mm(v_bank[i], "v", i, g)
-                for i in range(4):
-                    mm(qk_bank[i], "qk", i, g)
+        for g in range(PASSES - 2):
+            for i in range(4):
+                mm(qk_bank[i], "qk", i, g)
+                mm(v_bank[i], "v", i, g)
+        for i in range(4):
+            for g in range(PASSES - 2, PASSES):
+                mm(v_bank[i], "v", i, g)
+        for g in range(PASSES - 2, PASSES):
+            for i in range(4):
+                mm(qk_bank[i], "qk", i, g)
         for i in range(4):
             finish_v(v_bank[i], i)
         norms(qk_bank[0], 0)

@@ -58,7 +58,7 @@ TWO_PI = 2.0 * math.pi
 C1 = 6.28125
 C2 = TWO_PI - C1
 WARM_MATMULS = 22
-SPLIT = 8
+SPLIT = 10
 
 
 def tile_attentionhead_pa_kernel(tc, x_words, x_scales, W_qkv_words, W_qkv_scales, sqk, out_0, out_1, out_2):

@@ -19,46 +19,29 @@ D = 128
 HALF = 64
 ROPE_BASE = 10000.0
 
-LOADS = [
-    ("xc", 0, 0, 1),
-    ("wc", 0, 0, 1),
-    ("xs", 0, 0, 8),
-    ("ws", 0, 0, 16),
-    ("xc", 0, 1, 2),
-    ("wc", 0, 1, 2),
-    ("xc", 0, 2, 4),
-    ("wc", 0, 2, 4),
-    ("xc", 0, 4, 6),
-    ("wc", 0, 4, 6),
-    ("xc", 0, 6, 8),
-    ("wc", 0, 6, 8),
-    ("xs", 0, 8, 16),
-    ("xc", 0, 8, 10),
-    ("wc", 0, 8, 10),
-    ("xc", 0, 10, 12),
-    ("wc", 0, 10, 12),
-    ("xc", 0, 12, 14),
-    ("wc", 0, 12, 14),
-    ("xc", 0, 14, 16),
-    ("wc", 0, 14, 16),
-    ("xs", 1, 0, 8),
-    ("xc", 1, 0, 2),
-    ("xc", 1, 2, 4),
-    ("xc", 1, 4, 6),
-    ("xc", 1, 6, 8),
-    ("xs", 1, 8, 16),
-    ("xc", 1, 8, 10),
-    ("xc", 1, 10, 12),
-    ("xc", 1, 12, 14),
-    ("xc", 1, 14, 16),
-]
-VECTOR_ZEROS = 3
+ALL8 = 6
+SB = 10
+SC = 6
+JOINED = 6
+VECTOR_ZEROS = 2
 
 TWO_PI = 2.0 * math.pi
 C1 = 6.28125
 C2 = TWO_PI - C1
-WARM_MATMULS = 22
-SPLIT = 10
+WARM_MATMULS = 20
+
+
+def load_order():
+    order = [("xf", 0, 1), ("wc", 0, 1), ("xsf", 0, ALL8), ("ws", 0, ALL8), ("xf", 1, 2), ("wc", 1, 2)]
+    for g in range(2, ALL8, 2):
+        order += [("xf", g, g + 2), ("wc", g, g + 2)]
+    order += [("xs0", ALL8, PASSES), ("ws", ALL8, PASSES)]
+    for g in range(ALL8, PASSES, 2):
+        order += [("xc0", g, g + 2), ("wc", g, g + 2)]
+    order += [("xs1", ALL8, PASSES)]
+    for g in range(ALL8, PASSES, 2):
+        order += [("xc1", g, g + 2)]
+    return order
 
 
 def tile_attentionhead_pa_kernel(tc, x_words, x_scales, W_qkv_words, W_qkv_scales, sqk, out_0, out_1, out_2):
@@ -73,30 +56,14 @@ def tile_attentionhead_pa_kernel(tc, x_words, x_scales, W_qkv_words, W_qkv_scale
         psum = ctx.enter_context(tc.psum_pool(name="psum", bufs=1))
         ctx.enter_context(tc.manual_schedule())
 
-        x_codes = [{}, {}]
-        x_planes = [{}, {}]
-        wq_codes = {}
-        wv_codes = {}
-        w_planes = {}
-        widths = {"xc": 1024, "wc": 768, "wq": 512, "wv": 256, "xs": 512, "ws": 384}
+        widths = {"xf": 2048, "xc0": 1024, "xc1": 1024, "wc": 768, "xsf": 1024, "xs0": 512, "xs1": 512, "ws": 384}
+        where = {}
         loads = []
-        for kind, half, g0, g1 in LOADS:
-            t = keep.tile([P, g1 - g0, widths[kind]], U8, name="%s%d_%d" % (kind, half, g0), align_bytes=64)
-            loads.append((kind, half, g0, g1, t))
+        for kind, g0, g1 in load_order():
+            t = keep.tile([P, g1 - g0, widths[kind]], U8, name="%s_%d" % (kind, g0), align_bytes=64)
+            loads.append((kind, g0, g1, t))
             for g in range(g0, g1):
-                if kind == "xc":
-                    x_codes[half][g] = (t, g - g0)
-                elif kind == "xs":
-                    x_planes[half][g] = (t, g - g0)
-                elif kind == "ws":
-                    w_planes[g] = (t, g - g0)
-                elif kind == "wc":
-                    wq_codes[g] = (t, g - g0, 0)
-                    wv_codes[g] = (t, g - g0, 512)
-                elif kind == "wq":
-                    wq_codes[g] = (t, g - g0, 0)
-                else:
-                    wv_codes[g] = (t, g - g0, 0)
+                where[(kind, g)] = (t, g - g0)
 
         zero1 = keep.tile([P, 1], F32, name="zero1")
         junk1 = keep.tile([P, 1], F32, name="junk1")
@@ -120,7 +87,11 @@ def tile_attentionhead_pa_kernel(tc, x_words, x_scales, W_qkv_words, W_qkv_scale
         cos_t = keep.tile([P, 1024], F32, name="cos_t")
         sin_t = keep.tile([P, 1024], F32, name="sin_t")
 
-        planes = [entry[4] for entry in loads if entry[0] in ("xs", "ws")]
+        v_early = {}
+        for i in range(4, JOINED):
+            v_early[i] = keep.tile([P, D], F32, name="v_early%d" % i)
+
+        planes = [entry[3] for entry in loads if entry[0] in ("xsf", "xs0", "xs1", "ws")]
         for t in planes[:VECTOR_ZEROS]:
             nc.vector.memset(t[:].bitcast(I32), 0)
         nc.gpsimd.memset(ones[:], 1.0)
@@ -131,23 +102,27 @@ def tile_attentionhead_pa_kernel(tc, x_words, x_scales, W_qkv_words, W_qkv_scale
         for t in planes[VECTOR_ZEROS:]:
             nc.gpsimd.memset(t[:].bitcast(F32), 0.0)
 
-        for kind, half, a, b, t in loads:
-            if kind in ("xs", "ws"):
+        for kind, a, b, t in loads:
+            if kind in ("xsf", "xs0", "xs1", "ws"):
                 for r in range(4):
-                    if kind == "xs":
-                        src = x_scales[a:b, r:16:4, 512 * half : 512 * half + 512]
+                    if kind == "xsf":
+                        src = x_scales[a:b, r:16:4, :]
+                    elif kind == "xs0":
+                        src = x_scales[a:b, r:16:4, 0:512]
+                    elif kind == "xs1":
+                        src = x_scales[a:b, r:16:4, 512:1024]
                     else:
                         src = W_qkv_scales[a:b, r:16:4, :]
                     nc.sync.dma_start(out=t[r:P:32, :, :].bitcast(I32), in_=src.rearrange("g q c -> q g c").bitcast(I32))
             else:
-                if kind == "xc":
-                    src = x_words[a:b, :, 1024 * half : 1024 * half + 1024]
-                elif kind == "wc":
-                    src = W_qkv_words[a:b, :, :]
-                elif kind == "wq":
-                    src = W_qkv_words[a:b, :, 0:512]
+                if kind == "xf":
+                    src = x_words[a:b, :, :]
+                elif kind == "xc0":
+                    src = x_words[a:b, :, 0:1024]
+                elif kind == "xc1":
+                    src = x_words[a:b, :, 1024:2048]
                 else:
-                    src = W_qkv_words[a:b, :, 512:768]
+                    src = W_qkv_words[a:b, :, :]
                 nc.sync.dma_start(out=t[:].bitcast(I32), in_=src.rearrange("g p b -> p g b").bitcast(I32))
 
         nc.scalar.activation(out=junk1[:], in_=zero1[:], func=ACTF.Sin)
@@ -175,7 +150,7 @@ def tile_attentionhead_pa_kernel(tc, x_words, x_scales, W_qkv_words, W_qkv_scale
         nc.vector.tensor_scalar(out=c2[:], in0=q4[:], scalar1=-2.0, scalar2=1.0, op0=ALU.mult, op1=ALU.add)
         cos_v = cos_t[:].rearrange("p (t a h j) -> p t a h j", t=4, a=2, h=2)
         sin_v = sin_t[:].rearrange("p (t a h j) -> p t a h j", t=4, a=2, h=2)
-        nc.scalar.activation(out=junk1[:], in_=freq[:, 0:1], func=ACTF.Sqrt)
+        nc.scalar.activation(out=junk1[:], in_=freq[:, 0:1], func=ACTF.Abs_reciprocal_sqrt)
         nc.vector.tensor_scalar(out=cos1[:], in0=q2[:], scalar1=-2.0, scalar2=1.0, op0=ALU.mult, op1=ALU.add)
         nc.vector.scalar_tensor_tensor(out=sin1[:], in0=s2[:], scalar=2.0, in1=c2[:], op0=ALU.mult, op1=ALU.mult)
         for t in range(4):
@@ -185,122 +160,123 @@ def tile_attentionhead_pa_kernel(tc, x_words, x_scales, W_qkv_words, W_qkv_scale
         nc.vector.tensor_copy(out=cos_v[:, :, 1, :, :], in_=cos_v[:, :, 0, :, :])
         nc.vector.tensor_copy(out=sin_v[:, :, 1, :, :], in_=sin_v[:, :, 0, :, :])
 
-        def mm(bank, part, i, g):
-            half = i // 4
-            il = i % 4
-            xt, xl = x_codes[half][g]
-            st, sl = x_planes[half][g]
-            pt, pl = w_planes[g]
+        def mm(bank, part, i, g, o0, first, last):
+            if g < ALL8:
+                xt, xl = where[("xf", g)]
+                st, sl = where[("xsf", g)]
+                il = i
+            else:
+                xt, xl = where[("xc%d" % (i // 4), g)]
+                st, sl = where[("xs%d" % (i // 4), g)]
+                il = i % 4
+            wt, wl = where[("wc", g)]
+            pt, pl = where[("ws", g)]
             if part == "qk":
                 c0, c1 = 0, 256
-                wt, wl, wo = wq_codes[g]
             else:
                 c0, c1 = 256, 384
-                wt, wl, wo = wv_codes[g]
             nc.tensor.matmul_mx(
-                out=bank[:, 0 : c1 - c0],
+                out=bank[:, o0 : o0 + c1 - c0],
                 lhsT=xt[:, xl, 256 * il : 256 * (il + 1)].bitcast(FP4X4),
                 lhsT_scale=st[:, sl, P * il : P * (il + 1)],
-                rhs=wt[:, wl, wo : wo + 2 * (c1 - c0)].bitcast(FP4X4),
+                rhs=wt[:, wl, 2 * c0 : 2 * c1].bitcast(FP4X4),
                 rhs_scale=pt[:, pl, c0:c1],
-                start=(g == 0),
-                stop=(g == PASSES - 1),
+                start=first,
+                stop=last,
             )
 
-        def finish_v(bank, i):
-            vt = work.tile([P, D], F32, name="vt")
-            nc.scalar.copy(out=vt[:], in_=bank[:, 0:D])
-            nc.sync.dma_start(out=v_out[P * i : P * (i + 1), :], in_=vt[:])
+        def qk(i, g):
+            mm(bank[i], "qk", i, g, 0, g == 0, i >= 4 and g == PASSES - 1)
+
+        def v_joined(i, g):
+            mm(bank[i], "v", i, g, 256, False, i < 4 and g == PASSES - 1)
 
         state = {}
+        recip = {}
 
-        def norms(bank, i):
+        def norms(i):
             sq = work.tile([P, D], F32, name="sq")
             ss = work.tile([P, 2], F32, name="ss")
-            nc.scalar.activation(out=sq[:], in_=bank[:, 0:D], func=ACTF.Square, accum_out=ss[:, 0:1])
+            nc.scalar.activation(out=sq[:], in_=bank[i][:, 0:D], func=ACTF.Square, accum_out=ss[:, 0:1])
             sq_k = work.tile([P, D], F32, name="sq")
-            nc.scalar.activation(out=sq_k[:], in_=bank[:, D : 2 * D], func=ACTF.Square, accum_out=ss[:, 1:2])
-            nrm = work.tile([P, 2], F32, name="nrm")
-            nc.scalar.activation(out=nrm[:], in_=ss[:], func=ACTF.Sqrt)
-            state[i] = [nrm]
+            nc.scalar.activation(out=sq_k[:], in_=bank[i][:, D : 2 * D], func=ACTF.Square, accum_out=ss[:, 1:2])
+            rn = work.tile([P, 2], F32, name="rn")
+            nc.scalar.activation(out=rn[:], in_=ss[:], func=ACTF.Abs_reciprocal_sqrt)
+            recip[i] = rn
 
-        def rope(bank, i):
+        def rope_products(i):
             t = i % 4
-            nrm = state[i][0]
             t1 = work.tile([P, 256], F32, name="t1")
-            nc.vector.tensor_tensor(out=t1[:], in0=bank[:, 0:256], in1=cos_t[:, 256 * t : 256 * (t + 1)], op=ALU.mult)
+            nc.vector.tensor_tensor(out=t1[:], in0=bank[i][:, 0:256], in1=cos_t[:, 256 * t : 256 * (t + 1)], op=ALU.mult)
             t2 = work.tile([P, 256], F32, name="t2")
-            raw_v = bank[:, 0:256].rearrange("p (a h j) -> p a h j", a=2, h=2)
+            raw_v = bank[i][:, 0:256].rearrange("p (a h j) -> p a h j", a=2, h=2)
             t2_v = t2[:].rearrange("p (a h j) -> p a h j", a=2, h=2)
             nc.vector.tensor_tensor(out=t2_v[:, :, 0, :], in0=raw_v[:, :, 1, :], in1=sin_v[:, t, :, 0, :], op=ALU.mult)
             nc.vector.tensor_tensor(out=t2_v[:, :, 1, :], in0=raw_v[:, :, 0, :], in1=sin_v[:, t, :, 1, :], op=ALU.mult)
+            state[i] = [t1, t2]
+
+        def rope_add(i):
+            t1, t2 = state[i]
             sm = work.tile([P, 256], F32, name="sm")
             nc.vector.tensor_tensor(out=sm[:], in0=t1[:], in1=t2[:], op=ALU.add)
-            rn = work.tile([P, 2], F32, name="rn")
-            nc.vector.reciprocal(out=rn[:], in_=nrm[:])
-            state[i] = [sm, rn]
+            state[i] = sm
+
+        def v_copy(i):
+            if i < 4:
+                vt = work.tile([P, D], F32, name="vt")
+                nc.scalar.copy(out=vt[:], in_=bank[i][:, 256:384])
+                nc.sync.dma_start(out=v_out[P * i : P * (i + 1), :], in_=vt[:])
+            elif i < JOINED:
+                nc.scalar.copy(out=v_early[i][:], in_=bank[i][:, 256:384])
 
         def scale_store(i):
-            sm, rn = state[i]
+            sm = state[i]
+            rn = recip[i]
             res = work.tile([P, 256], F32, name="res")
             nc.scalar.activation(out=res[:, 0:D], in_=sm[:, 0:D], func=ACTF.Copy, scale=rn[:, 0:1])
             nc.scalar.activation(out=res[:, D : 2 * D], in_=sm[:, D : 2 * D], func=ACTF.Copy, scale=rn[:, 1:2])
             nc.sync.dma_start(out=q_out[P * i : P * (i + 1), :], in_=res[:, 0:D])
             nc.sync.dma_start(out=k_out[P * i : P * (i + 1), :], in_=res[:, D : 2 * D])
 
-        def new_bank(b):
-            bank = psum.tile([P, 512], F32, name="bank%d" % b)
-            return bank
+        bank = {}
+        for i in range(8):
+            bank[i] = psum.tile([P, 512], F32, name="bank%d" % i)
 
-        qk_bank = {}
-        v_bank = {}
-        for i in range(4):
-            qk_bank[i] = new_bank(i)
-            v_bank[i] = new_bank(4 + i)
-        for g in range(PASSES - 2):
+        for g in range(ALL8):
+            for i in range(8):
+                qk(i, g)
+                if i < JOINED:
+                    v_joined(i, g)
+        for g in range(ALL8, SB):
             for i in range(4):
-                mm(qk_bank[i], "qk", i, g)
-                mm(v_bank[i], "v", i, g)
+                qk(i, g)
+                v_joined(i, g)
         for i in range(4):
-            for g in range(PASSES - 2, PASSES):
-                mm(v_bank[i], "v", i, g)
-        for g in range(PASSES - 2, PASSES):
-            for i in range(4):
-                mm(qk_bank[i], "qk", i, g)
-        for i in range(4):
-            finish_v(v_bank[i], i)
-        norms(qk_bank[0], 0)
-        for i in range(4):
-            if i < 3:
-                norms(qk_bank[i + 1], i + 1)
-            rope(qk_bank[i], i)
+            for g in range(SB, PASSES):
+                qk(i, g)
+                v_joined(i, g)
+        for g in range(ALL8, SC):
+            for i in range(4, 8):
+                qk(i, g)
+        for i in range(4, 8):
+            for g in range(SC, PASSES):
+                qk(i, g)
+
+        for i in range(8):
+            rope_products(i)
+            norms(i)
+            rope_add(i)
+            v_copy(i)
             scale_store(i)
 
         for i in range(4, 8):
-            qk_bank[i] = new_bank(i)
-        for g in range(SPLIT):
-            for i in range(4, 8):
-                mm(qk_bank[i], "qk", i, g)
-        for i in range(4, 8):
-            for g in range(SPLIT, PASSES):
-                mm(qk_bank[i], "qk", i, g)
-        for i in range(4, 8):
-            v_bank[i] = new_bank(i - 4)
-            for g in range(PASSES):
-                mm(v_bank[i], "v", i, g)
-        norms(qk_bank[4], 4)
-        norms(qk_bank[5], 5)
-        rope(qk_bank[4], 4)
-        scale_store(4)
-        norms(qk_bank[6], 6)
-        rope(qk_bank[5], 5)
-        scale_store(5)
-        norms(qk_bank[7], 7)
-        finish_v(v_bank[4], 4)
-        rope(qk_bank[6], 6)
-        scale_store(6)
-        finish_v(v_bank[5], 5)
-        rope(qk_bank[7], 7)
-        scale_store(7)
-        finish_v(v_bank[6], 6)
-        finish_v(v_bank[7], 7)
+            late = psum.tile([P, 512], F32, name="bank%d" % (i - 4))
+            g0 = ALL8 if i < JOINED else 0
+            for g in range(g0, PASSES):
+                mm(late, "v", i, g, 0, g == g0, g == PASSES - 1)
+            vt = work.tile([P, D], F32, name="vt")
+            if i < JOINED:
+                nc.vector.tensor_tensor(out=vt[:], in0=late[:, 0:D], in1=v_early[i][:], op=ALU.add)
+            else:
+                nc.scalar.copy(out=vt[:], in_=late[:, 0:D])
+            nc.sync.dma_start(out=v_out[P * i : P * (i + 1), :], in_=vt[:])

@@ -186,10 +186,37 @@ def tile_attentionhead_pa_kernel(tc, x_words, x_scales, W_qkv_words, W_qkv_scale
             )
 
         def qk(i, g):
-            mm(bank[i], "qk", i, g, 0, g == 0, i >= 4 and g == PASSES - 1)
+            mm(bank[i], "qk", i, g, 0, g == 0, (i >= 4 or i % 2 == 1) and g == PASSES - 1)
 
         def v_joined(i, g):
-            mm(bank[i], "v", i, g, 256, False, i < 4 and g == PASSES - 1)
+            mm(bank[i], "v", i, g, 256, False, False)
+
+        def v_turned(j, g):
+            if g < ALL8:
+                xt, xl = where[("xf", g)]
+                st, sl = where[("xsf", g)]
+            else:
+                xt, xl = where[("xc0", g)]
+                st, sl = where[("xs0", g)]
+            wt, wl = where[("wc", g)]
+            pt, pl = where[("ws", g)]
+            nc.tensor.matmul_mx(
+                out=bank[2 * j][:, 256:512],
+                lhsT=wt[:, wl, 512:768].bitcast(FP4X4),
+                lhsT_scale=pt[:, pl, 256:384],
+                rhs=xt[:, xl, 512 * j : 512 * (j + 1)].bitcast(FP4X4),
+                rhs_scale=st[:, sl, 256 * j : 256 * (j + 1)],
+                start=False,
+                stop=(g == PASSES - 1),
+            )
+
+        def step(i, g):
+            qk(i, g)
+            if i < 4:
+                if i % 2 == 0:
+                    v_turned(i // 2, g)
+            elif i < JOINED and g < ALL8:
+                v_joined(i, g)
 
         state = {}
         recip = {}
@@ -223,9 +250,15 @@ def tile_attentionhead_pa_kernel(tc, x_words, x_scales, W_qkv_words, W_qkv_scale
 
         def v_copy(i):
             if i < 4:
-                vt = work.tile([P, D], F32, name="vt")
-                nc.scalar.copy(out=vt[:], in_=bank[i][:, 256:384])
-                nc.sync.dma_start(out=v_out[P * i : P * (i + 1), :], in_=vt[:])
+                if i % 2 == 0:
+                    turned = work.tile([P, 256], F32, name="turned", align_bytes=64)
+                    nc.vector.transpose(out=turned[:, 0:128], in_=bank[i][:, 256:384])
+                    nc.vector.transpose(out=turned[:, 128:256], in_=bank[i][:, 384:512])
+                    for c in range(4):
+                        nc.sync.dma_start(
+                            out=v_out[P * i : P * (i + 2), 32 * c : 32 * (c + 1)].rearrange("(n a) b -> a n b", a=32),
+                            in_=turned[32 * c : 32 * (c + 1), :].rearrange("p (n b) -> p n b", b=32),
+                        )
             elif i < JOINED:
                 nc.scalar.copy(out=v_early[i][:], in_=bank[i][:, 256:384])
 
@@ -244,17 +277,13 @@ def tile_attentionhead_pa_kernel(tc, x_words, x_scales, W_qkv_words, W_qkv_scale
 
         for g in range(ALL8):
             for i in range(8):
-                qk(i, g)
-                if i < JOINED:
-                    v_joined(i, g)
+                step(i, g)
         for g in range(ALL8, SB):
             for i in range(4):
-                qk(i, g)
-                v_joined(i, g)
+                step(i, g)
         for i in range(4):
             for g in range(SB, PASSES):
-                qk(i, g)
-                v_joined(i, g)
+                step(i, g)
         for g in range(ALL8, SC):
             for i in range(4, 8):
                 qk(i, g)

@@ -92,11 +92,11 @@ def tile_attentionhead_pa_kernel(tc, x_words, x_scales, W_qkv_words, W_qkv_scale
             v_early[i] = keep.tile([P, D], F32, name="v_early%d" % i)
 
         planes = [entry[3] for entry in loads if entry[0] in ("xsf", "xs0", "xs1", "ws")]
+        nc.vector.memset(ones[:], 1.0)
         for t in planes[:VECTOR_ZEROS]:
             nc.vector.memset(t[:].bitcast(I32), 0)
-        nc.gpsimd.memset(ones[:], 1.0)
-        nc.gpsimd.memset(zero1[:], 0.0)
-        nc.gpsimd.memset(g_row[:], 0.0)
+        nc.vector.memset(zero1[:], 0.0)
+        nc.vector.memset(g_row[:], 0.0)
         nc.gpsimd.dma_start(out=g_row[0:1, :], in_=sqk.rearrange("(o d) -> o d", o=1))
         nc.gpsimd.iota(pos_i[:], pattern=[[P, 4]], base=0, channel_multiplier=1)
         for t in planes[VECTOR_ZEROS:]:

@@ -32,15 +32,16 @@ WARM_MATMULS = 20
 
 
 def load_order():
-    order = [("xf", 0, 1), ("wc", 0, 1), ("xsf", 0, ALL8), ("ws", 0, ALL8), ("xf", 1, 2), ("wc", 1, 2)]
+    every = (0, 1, 2, 3)
+    order = [("xf", 0, 1, ()), ("wc", 0, 1, ()), ("ws", 0, ALL8, (0, 1)), ("xsf", 0, ALL8, every), ("ws", 0, ALL8, (2, 3)), ("xf", 1, 2, ()), ("wc", 1, 2, ())]
     for g in range(2, ALL8, 2):
-        order += [("xf", g, g + 2), ("wc", g, g + 2)]
-    order += [("xs0", ALL8, PASSES), ("ws", ALL8, PASSES)]
+        order += [("xf", g, g + 2, ()), ("wc", g, g + 2, ())]
+    order += [("xs0", ALL8, PASSES, every), ("ws", ALL8, PASSES, every)]
     for g in range(ALL8, PASSES, 2):
-        order += [("xc0", g, g + 2), ("wc", g, g + 2)]
-    order += [("xs1", ALL8, PASSES)]
+        order += [("xc0", g, g + 2, ()), ("wc", g, g + 2, ())]
+    order += [("xs1", ALL8, PASSES, every)]
     for g in range(ALL8, PASSES, 2):
-        order += [("xc1", g, g + 2)]
+        order += [("xc1", g, g + 2, ())]
     return order
 
 
@@ -59,9 +60,15 @@ def tile_attentionhead_pa_kernel(tc, x_words, x_scales, W_qkv_words, W_qkv_scale
         widths = {"xf": 2048, "xc0": 1024, "xc1": 1024, "wc": 768, "xsf": 1024, "xs0": 512, "xs1": 512, "ws": 384}
         where = {}
         loads = []
-        for kind, g0, g1 in load_order():
-            t = keep.tile([P, g1 - g0, widths[kind]], U8, name="%s_%d" % (kind, g0), align_bytes=64)
-            loads.append((kind, g0, g1, t))
+        planes = []
+        for kind, g0, g1, rows in load_order():
+            if (kind, g0) in where:
+                t = where[(kind, g0)][0]
+            else:
+                t = keep.tile([P, g1 - g0, widths[kind]], U8, name="%s_%d" % (kind, g0), align_bytes=64)
+                if len(rows) > 0:
+                    planes.append(t)
+            loads.append((kind, g0, g1, rows, t))
             for g in range(g0, g1):
                 where[(kind, g)] = (t, g - g0)
 
@@ -91,7 +98,6 @@ def tile_attentionhead_pa_kernel(tc, x_words, x_scales, W_qkv_words, W_qkv_scale
         for i in range(4, JOINED):
             v_early[i] = keep.tile([P, D], F32, name="v_early%d" % i)
 
-        planes = [entry[3] for entry in loads if entry[0] in ("xsf", "xs0", "xs1", "ws")]
         nc.vector.memset(ones[:], 1.0)
         for t in planes[:VECTOR_ZEROS]:
             nc.vector.memset(t[:].bitcast(I32), 0)
@@ -102,9 +108,9 @@ def tile_attentionhead_pa_kernel(tc, x_words, x_scales, W_qkv_words, W_qkv_scale
         for t in planes[VECTOR_ZEROS:]:
             nc.gpsimd.memset(t[:].bitcast(F32), 0.0)
 
-        for kind, a, b, t in loads:
-            if kind in ("xsf", "xs0", "xs1", "ws"):
-                for r in range(4):
+        for kind, a, b, rows, t in loads:
+            if len(rows) > 0:
+                for r in rows:
                     if kind == "xsf":
                         src = x_scales[a:b, r:16:4, :]
                     elif kind == "xs0":

@@ -20,7 +20,7 @@ HALF = 64
 ROPE_BASE = 10000.0
 
 ALL8 = 6
-SB = 10
+SB = 8
 SC = 6
 JOINED = 6
 VECTOR_ZEROS = 2
@@ -244,8 +244,7 @@ def tile_attentionhead_pa_kernel(tc, x_words, x_scales, W_qkv_words, W_qkv_scale
             t2 = work.tile([P, 256], F32, name="t2")
             raw_v = bank[i][:, 0:256].rearrange("p (a h j) -> p a h j", a=2, h=2)
             t2_v = t2[:].rearrange("p (a h j) -> p a h j", a=2, h=2)
-            nc.vector.tensor_tensor(out=t2_v[:, :, 0, :], in0=raw_v[:, :, 1, :], in1=sin_v[:, t, :, 0, :], op=ALU.mult)
-            nc.vector.tensor_tensor(out=t2_v[:, :, 1, :], in0=raw_v[:, :, 0, :], in1=sin_v[:, t, :, 1, :], op=ALU.mult)
+            nc.vector.tensor_tensor(out=t2_v[:, :, :, :], in0=raw_v[:, :, ::-1, :], in1=sin_v[:, t, :, :, :], op=ALU.mult)
             state[i] = [t1, t2]
 
         def rope_add(i):

@@ -57,7 +57,7 @@ def tile_attentionhead_pa_kernel(tc, x_words, x_scales, W_qkv_words, W_qkv_scale
         psum = ctx.enter_context(tc.psum_pool(name="psum", bufs=1))
         ctx.enter_context(tc.manual_schedule())
 
-        widths = {"xf": 2048, "xc0": 1024, "xc1": 1024, "wc": 768, "xsf": 1024, "xs0": 512, "xs1": 512, "ws": 384}
+        widths = {"xf": 2048, "xc0": 1024, "xc1": 1024, "wc": 768, "xsf": 1024, "xs0": 512, "xs1": 512, "ws": 512}
         where = {}
         loads = []
         planes = []
@@ -65,7 +65,7 @@ def tile_attentionhead_pa_kernel(tc, x_words, x_scales, W_qkv_words, W_qkv_scale
             if (kind, g0) in where:
                 t = where[(kind, g0)][0]
             else:
-                t = keep.tile([P, g1 - g0, widths[kind]], U8, name="%s_%d" % (kind, g0), align_bytes=64)
+                t = keep.tile([P, g1 - g0, widths[kind]], U8, name="%s_%d" % (kind, g0), align_bytes=256)
                 if len(rows) > 0:
                     planes.append(t)
             loads.append((kind, g0, g1, rows, t))
@@ -119,7 +119,8 @@ def tile_attentionhead_pa_kernel(tc, x_words, x_scales, W_qkv_words, W_qkv_scale
                         src = x_scales[a:b, r:16:4, 512:1024]
                     else:
                         src = W_qkv_scales[a:b, r:16:4, :]
-                    nc.sync.dma_start(out=t[r:P:32, :, :].bitcast(I32), in_=src.rearrange("g q c -> q g c").bitcast(I32))
+                    wide = 384 if kind == "ws" else widths[kind]
+                    nc.sync.dma_start(out=t[r:P:32, :, 0:wide].bitcast(I32), in_=src.rearrange("g q c -> q g c").bitcast(I32))
             else:
                 if kind == "xf":
                     src = x_words[a:b, :, :]

@@ -57,7 +57,7 @@ def tile_attentionhead_pa_kernel(tc, x_words, x_scales, W_qkv_words, W_qkv_scale
         psum = ctx.enter_context(tc.psum_pool(name="psum", bufs=1))
         ctx.enter_context(tc.manual_schedule())
 
-        widths = {"xf": 2048, "xc0": 1024, "xc1": 1024, "wc": 768, "xsf": 1024, "xs0": 512, "xs1": 512, "ws": 512}
+        widths = {"xf": 2048, "xc0": 1024, "xc1": 1024, "wc": 1024, "xsf": 1024, "xs0": 512, "xs1": 512, "ws": 512}
         where = {}
         loads = []
         planes = []
@@ -130,7 +130,8 @@ def tile_attentionhead_pa_kernel(tc, x_words, x_scales, W_qkv_words, W_qkv_scale
                     src = x_words[a:b, :, 1024:2048]
                 else:
                     src = W_qkv_words[a:b, :, :]
-                nc.sync.dma_start(out=t[:].bitcast(I32), in_=src.rearrange("g p b -> p g b").bitcast(I32))
+                wide = 768 if kind == "wc" else widths[kind]
+                nc.sync.dma_start(out=t[:, :, 0:wide].bitcast(I32), in_=src.rearrange("g p b -> p g b").bitcast(I32))
 
         nc.scalar.activation(out=junk1[:], in_=zero1[:], func=ACTF.Sin)
         g_ps = psum.tile([P, 512], F32, name="bank7")

@@ -23,17 +23,19 @@ ALL8 = 6
 SB = 8
 SC = 6
 JOINED = 6
-VECTOR_ZEROS = 2
+VECTOR_ZEROS = 3
+XS_FIRST = 2
+LATE = 2
 
 TWO_PI = 2.0 * math.pi
 C1 = 6.28125
 C2 = TWO_PI - C1
-WARM_MATMULS = 20
+WARM_MATMULS = 14
 
 
 def load_order():
     every = (0, 1, 2, 3)
-    order = [("xf", 0, 1, ()), ("wc", 0, 1, ()), ("ws", 0, ALL8, (0, 1)), ("xsf", 0, ALL8, every), ("ws", 0, ALL8, (2, 3)), ("xf", 1, 2, ()), ("wc", 1, 2, ())]
+    order = [("xf", 0, 1, ()), ("wc", 0, 1, ()), ("ws", 0, ALL8, (0, 1)), ("xsf", 0, XS_FIRST, every), ("ws", 0, ALL8, (2, 3)), ("xf", 1, 2, ()), ("wc", 1, 2, ()), ("xsf", XS_FIRST, ALL8, every)]
     for g in range(2, ALL8, 2):
         order += [("xf", g, g + 2, ()), ("wc", g, g + 2, ())]
     order += [("xs0", ALL8, PASSES, every), ("ws", ALL8, PASSES, every)]
@@ -137,37 +139,6 @@ def tile_attentionhead_pa_kernel(tc, x_words, x_scales, W_qkv_words, W_qkv_scale
         g_ps = psum.tile([P, 512], F32, name="bank7")
         for n in range(WARM_MATMULS):
             nc.tensor.matmul(out=g_ps[:], lhsT=ones[:, 0:P], rhs=ones[:], start=True, stop=True)
-        nc.tensor.matmul(out=g_ps[:, 0:D], lhsT=ones[:, 0:P], rhs=g_row[:], start=True, stop=True)
-        nc.scalar.copy(out=gain[:], in_=g_ps[:, 0:D])
-
-        nc.vector.memset(freq[:, 0:1], 1.0)
-        w = 1
-        while w < HALF:
-            nc.vector.tensor_scalar(out=freq[:, w : 2 * w], in0=freq[:, 0:w], scalar1=ROPE_BASE ** (-w / 64.0), scalar2=None, op0=ALU.mult)
-            w *= 2
-        nc.vector.tensor_copy(out=pos_f[:], in_=pos_i[:])
-        for t in range(4):
-            nc.vector.tensor_scalar(out=ang[:, HALF * t : HALF * (t + 1)], in0=freq[:], scalar1=pos_f[:, t : t + 1], scalar2=None, op0=ALU.mult)
-        nc.vector.tensor_scalar(out=turns[:], in0=ang[:], scalar1=1.0 / TWO_PI, scalar2=0.25, op0=ALU.mult, op1=ALU.add)
-        nc.vector.scalar_tensor_tensor(out=red1[:], in0=turns[:], scalar=-C1, in1=ang[:], op0=ALU.mult, op1=ALU.add)
-        nc.vector.scalar_tensor_tensor(out=red[:], in0=turns[:], scalar=-C2, in1=red1[:], op0=ALU.mult, op1=ALU.add)
-        nc.scalar.activation(out=s4[:], in_=red[:], func=ACTF.Sin, scale=0.25)
-        nc.scalar.activation(out=s2[:], in_=red[:], func=ACTF.Sin, scale=0.5)
-        nc.scalar.activation(out=q4[:], in_=s4[:], func=ACTF.Square)
-        nc.scalar.activation(out=q2[:], in_=s2[:], func=ACTF.Square)
-        nc.vector.tensor_scalar(out=c2[:], in0=q4[:], scalar1=-2.0, scalar2=1.0, op0=ALU.mult, op1=ALU.add)
-        cos_v = cos_t[:].rearrange("p (t a h j) -> p t a h j", t=4, a=2, h=2)
-        sin_v = sin_t[:].rearrange("p (t a h j) -> p t a h j", t=4, a=2, h=2)
-        nc.scalar.activation(out=junk1[:], in_=freq[:, 0:1], func=ACTF.Abs_reciprocal_sqrt)
-        nc.vector.tensor_scalar(out=cos1[:], in0=q2[:], scalar1=-2.0, scalar2=1.0, op0=ALU.mult, op1=ALU.add)
-        nc.vector.scalar_tensor_tensor(out=sin1[:], in0=s2[:], scalar=2.0, in1=c2[:], op0=ALU.mult, op1=ALU.mult)
-        for t in range(4):
-            for h in range(2):
-                nc.vector.tensor_tensor(out=cos_v[:, t, 0, h, :], in0=cos1[:, HALF * t : HALF * (t + 1)], in1=gain[:, HALF * h : HALF * (h + 1)], op=ALU.mult)
-                nc.vector.scalar_tensor_tensor(out=sin_v[:, t, 0, h, :], in0=sin1[:, HALF * t : HALF * (t + 1)], scalar=(-1.0 if h == 0 else 1.0), in1=gain[:, HALF * h : HALF * (h + 1)], op0=ALU.mult, op1=ALU.mult)
-        nc.vector.tensor_copy(out=cos_v[:, :, 1, :, :], in_=cos_v[:, :, 0, :, :])
-        nc.vector.tensor_copy(out=sin_v[:, :, 1, :, :], in_=sin_v[:, :, 0, :, :])
-
         def mm(bank, part, i, g, o0, first, last):
             if g < ALL8:
                 xt, xl = where[("xf", g)]
@@ -194,7 +165,7 @@ def tile_attentionhead_pa_kernel(tc, x_words, x_scales, W_qkv_words, W_qkv_scale
             )
 
         def qk(i, g):
-            mm(bank[i], "qk", i, g, 0, g == 0, (i >= 4 or i % 2 == 1) and g == PASSES - 1)
+            mm(bank[i], "qk", i, g, 0, g == (LATE if i == 7 else 0), (i >= 4 or i % 2 == 1) and g == PASSES - 1)
 
         def v_joined(i, g):
             mm(bank[i], "v", i, g, 256, False, False)
@@ -279,12 +250,51 @@ def tile_attentionhead_pa_kernel(tc, x_words, x_scales, W_qkv_words, W_qkv_scale
             nc.sync.dma_start(out=k_out[P * i : P * (i + 1), :], in_=res[:, D : 2 * D])
 
         bank = {}
-        for i in range(8):
+        for i in range(7):
             bank[i] = psum.tile([P, 512], F32, name="bank%d" % i)
 
-        for g in range(ALL8):
+        for g in range(LATE):
+            for i in range(7):
+                step(i, g)
+
+        nc.tensor.matmul(out=g_ps[:, 0:D], lhsT=ones[:, 0:P], rhs=g_row[:], start=True, stop=True)
+        nc.scalar.copy(out=gain[:], in_=g_ps[:, 0:D])
+
+        nc.vector.memset(freq[:, 0:1], 1.0)
+        w = 1
+        while w < HALF:
+            nc.vector.tensor_scalar(out=freq[:, w : 2 * w], in0=freq[:, 0:w], scalar1=ROPE_BASE ** (-w / 64.0), scalar2=None, op0=ALU.mult)
+            w *= 2
+        nc.vector.tensor_copy(out=pos_f[:], in_=pos_i[:])
+        for t in range(4):
+            nc.vector.tensor_scalar(out=ang[:, HALF * t : HALF * (t + 1)], in0=freq[:], scalar1=pos_f[:, t : t + 1], scalar2=None, op0=ALU.mult)
+        nc.vector.tensor_scalar(out=turns[:], in0=ang[:], scalar1=1.0 / TWO_PI, scalar2=0.25, op0=ALU.mult, op1=ALU.add)
+        nc.vector.scalar_tensor_tensor(out=red1[:], in0=turns[:], scalar=-C1, in1=ang[:], op0=ALU.mult, op1=ALU.add)
+        nc.vector.scalar_tensor_tensor(out=red[:], in0=turns[:], scalar=-C2, in1=red1[:], op0=ALU.mult, op1=ALU.add)
+        nc.scalar.activation(out=s4[:], in_=red[:], func=ACTF.Sin, scale=0.25)
+        nc.scalar.activation(out=s2[:], in_=red[:], func=ACTF.Sin, scale=0.5)
+        nc.scalar.activation(out=q4[:], in_=s4[:], func=ACTF.Square)
+        nc.scalar.activation(out=q2[:], in_=s2[:], func=ACTF.Square)
+        nc.vector.tensor_scalar(out=c2[:], in0=q4[:], scalar1=-2.0, scalar2=1.0, op0=ALU.mult, op1=ALU.add)
+        cos_v = cos_t[:].rearrange("p (t a h j) -> p t a h j", t=4, a=2, h=2)
+        sin_v = sin_t[:].rearrange("p (t a h j) -> p t a h j", t=4, a=2, h=2)
+        nc.scalar.activation(out=junk1[:], in_=freq[:, 0:1], func=ACTF.Abs_reciprocal_sqrt)
+        nc.vector.tensor_scalar(out=cos1[:], in0=q2[:], scalar1=-2.0, scalar2=1.0, op0=ALU.mult, op1=ALU.add)
+        nc.vector.scalar_tensor_tensor(out=sin1[:], in0=s2[:], scalar=2.0, in1=c2[:], op0=ALU.mult, op1=ALU.mult)
+        for t in range(4):
+            for h in range(2):
+                nc.vector.tensor_tensor(out=cos_v[:, t, 0, h, :], in0=cos1[:, HALF * t : HALF * (t + 1)], in1=gain[:, HALF * h : HALF * (h + 1)], op=ALU.mult)
+                nc.vector.scalar_tensor_tensor(out=sin_v[:, t, 0, h, :], in0=sin1[:, HALF * t : HALF * (t + 1)], scalar=(-1.0 if h == 0 else 1.0), in1=gain[:, HALF * h : HALF * (h + 1)], op0=ALU.mult, op1=ALU.mult)
+        nc.vector.tensor_copy(out=cos_v[:, :, 1, :, :], in_=cos_v[:, :, 0, :, :])
+        nc.vector.tensor_copy(out=sin_v[:, :, 1, :, :], in_=sin_v[:, :, 0, :, :])
+
+
+        bank[7] = psum.tile([P, 512], F32, name="bank7")
+        for g in range(LATE, ALL8):
             for i in range(8):
                 step(i, g)
+        for g in range(LATE):
+            step(7, g)
         for g in range(ALL8, SB):
             for i in range(4):
                 step(i, g)

@@ -24,7 +24,7 @@ SB = 8
 SC = 6
 JOINED = 6
 VECTOR_ZEROS = 3
-XS_FIRST = 2
+XS_FIRST = 3
 LATE = 2
 
 TWO_PI = 2.0 * math.pi
@@ -35,9 +35,8 @@ WARM_MATMULS = 14
 
 def load_order():
     every = (0, 1, 2, 3)
-    order = [("xf", 0, 1, ()), ("wc", 0, 1, ()), ("ws", 0, ALL8, (0, 1)), ("xsf", 0, XS_FIRST, every), ("ws", 0, ALL8, (2, 3)), ("xf", 1, 2, ()), ("wc", 1, 2, ()), ("xsf", XS_FIRST, ALL8, every)]
-    for g in range(2, ALL8, 2):
-        order += [("xf", g, g + 2, ()), ("wc", g, g + 2, ())]
+    order = [("xf", 0, 1, ()), ("wc", 0, 1, ()), ("ws", 0, ALL8, (0, 1)), ("xsf", 0, XS_FIRST, every), ("ws", 0, ALL8, (2, 3))]
+    order += [("xf", 1, 3, ()), ("wc", 1, 3, ()), ("xf", 3, 5, ()), ("wc", 3, 5, ()), ("xsf", XS_FIRST, ALL8, every), ("xf", 5, ALL8, ()), ("wc", 5, ALL8, ())]
     order += [("xs0", ALL8, PASSES, every), ("ws", ALL8, PASSES, every)]
     for g in range(ALL8, PASSES, 2):
         order += [("xc0", g, g + 2, ()), ("wc", g, g + 2, ())]

@@ -21,6 +21,7 @@ ROPE_BASE = 10000.0
 
 ALL8 = 6
 SB = 8
+TURN = 12
 SC = 6
 JOINED = 6
 VECTOR_ZEROS = 3
@@ -297,7 +298,11 @@ def tile_attentionhead_pa_kernel(tc, x_words, x_scales, W_qkv_words, W_qkv_scale
         for g in range(ALL8, SB):
             for i in range(4):
                 step(i, g)
-        for i in range(4):
+        for g0, g1 in ((SB, TURN), (TURN, PASSES)):
+            for i in range(2):
+                for g in range(g0, g1):
+                    step(i, g)
+        for i in range(2, 4):
             for g in range(SB, PASSES):
                 step(i, g)
         for g in range(ALL8, SC):

@@ -37,7 +37,7 @@ WARM_MATMULS = 14
 def load_order():
     every = (0, 1, 2, 3)
     order = [("xf", 0, 1, ()), ("wc", 0, 1, ()), ("ws", 0, ALL8, (0, 1)), ("xsf", 0, XS_FIRST, every), ("ws", 0, ALL8, (2, 3))]
-    order += [("xf", 1, 3, ()), ("wc", 1, 3, ()), ("xf", 3, 5, ()), ("wc", 3, 5, ()), ("xsf", XS_FIRST, ALL8, every), ("xf", 5, ALL8, ()), ("wc", 5, ALL8, ())]
+    order += [("xf", 1, 2, ()), ("wc", 1, 2, ()), ("xf", 2, 4, ()), ("wc", 2, 4, ()), ("xsf", XS_FIRST, ALL8, every), ("xf", 4, ALL8, ()), ("wc", 4, ALL8, ())]
     order += [("xs0", ALL8, PASSES, every), ("ws", ALL8, PASSES, every)]
     for g in range(ALL8, PASSES, 2):
         order += [("xc0", g, g + 2, ()), ("wc", g, g + 2, ())]

@@ -24,9 +24,9 @@ SB = 8
 TURN = 12
 SC = 6
 JOINED = 6
-VECTOR_ZEROS = 3
+VECTOR_ZEROS = 5
 XS_FIRST = 3
-LATE = 2
+LATE = 3
 
 TWO_PI = 2.0 * math.pi
 C1 = 6.28125

@@ -36,8 +36,8 @@ WARM_MATMULS = 14
 
 def load_order():
     every = (0, 1, 2, 3)
-    order = [("xf", 0, 1, ()), ("wc", 0, 1, ()), ("ws", 0, ALL8, (0, 1)), ("xsf", 0, XS_FIRST, every), ("ws", 0, ALL8, (2, 3))]
-    order += [("xf", 1, 2, ()), ("wc", 1, 2, ()), ("xf", 2, 4, ()), ("wc", 2, 4, ()), ("xsf", XS_FIRST, ALL8, every), ("xf", 4, ALL8, ()), ("wc", 4, ALL8, ())]
+    order = [("wc", 0, 1, ()), ("xc0", 0, 1, ()), ("ws", 0, ALL8, (0, 1)), ("xsf", 0, XS_FIRST, every), ("ws", 0, ALL8, (2, 3))]
+    order += [("xc1", 0, 1, ()), ("xf", 1, 2, ()), ("wc", 1, 2, ()), ("xf", 2, 4, ()), ("wc", 2, 4, ()), ("xsf", XS_FIRST, ALL8, every), ("xf", 4, ALL8, ()), ("wc", 4, ALL8, ())]
     order += [("xs0", ALL8, PASSES, every), ("ws", ALL8, PASSES, every)]
     for g in range(ALL8, PASSES, 2):
         order += [("xc0", g, g + 2, ()), ("wc", g, g + 2, ())]
@@ -140,12 +140,16 @@ def tile_attentionhead_pa_kernel(tc, x_words, x_scales, W_qkv_words, W_qkv_scale
         for n in range(WARM_MATMULS):
             nc.tensor.matmul(out=g_ps[:], lhsT=ones[:, 0:P], rhs=ones[:], start=True, stop=True)
         def mm(bank, part, i, g, o0, first, last):
-            if g < ALL8:
+            if ("xf", g) in where:
                 xt, xl = where[("xf", g)]
+                cl = i
+            else:
+                xt, xl = where[("xc%d" % (i // 4), g)]
+                cl = i % 4
+            if g < ALL8:
                 st, sl = where[("xsf", g)]
                 il = i
             else:
-                xt, xl = where[("xc%d" % (i // 4), g)]
                 st, sl = where[("xs%d" % (i // 4), g)]
                 il = i % 4
             wt, wl = where[("wc", g)]
@@ -156,7 +160,7 @@ def tile_attentionhead_pa_kernel(tc, x_words, x_scales, W_qkv_words, W_qkv_scale
                 c0, c1 = 256, 384
             nc.tensor.matmul_mx(
                 out=bank[:, o0 : o0 + c1 - c0],
-                lhsT=xt[:, xl, 256 * il : 256 * (il + 1)].bitcast(FP4X4),
+                lhsT=xt[:, xl, 256 * cl : 256 * (cl + 1)].bitcast(FP4X4),
                 lhsT_scale=st[:, sl, P * il : P * (il + 1)],
                 rhs=wt[:, wl, 2 * c0 : 2 * c1].bitcast(FP4X4),
                 rhs_scale=pt[:, pl, c0:c1],
@@ -171,11 +175,13 @@ def tile_attentionhead_pa_kernel(tc, x_words, x_scales, W_qkv_words, W_qkv_scale
             mm(bank[i], "v", i, g, 256, False, False)
 
         def v_turned(j, g):
-            if g < ALL8:
+            if ("xf", g) in where:
                 xt, xl = where[("xf", g)]
-                st, sl = where[("xsf", g)]
             else:
                 xt, xl = where[("xc0", g)]
+            if g < ALL8:
+                st, sl = where[("xsf", g)]
+            else:
                 st, sl = where[("xs0", g)]
             wt, wl = where[("wc", g)]
             pt, pl = where[("ws", g)]

@@ -321,9 +321,13 @@ def tile_attentionhead_pa_kernel(tc, x_words, x_scales, W_qkv_words, W_qkv_scale
         for i in range(8):
             rope_products(i)
             norms(i)
-            rope_add(i)
-            v_copy(i)
-            scale_store(i)
+            if i > 0:
+                rope_add(i - 1)
+                v_copy(i - 1)
+                scale_store(i - 1)
+        rope_add(7)
+        v_copy(7)
+        scale_store(7)
 
         for i in range(4, 8):
             late = psum.tile([P, 512], F32, name="bank%d" % (i - 4))

from contextlib import ExitStack
import math

import concourse.mybir as mybir

FLOPS = 2 * 1024 * 8192 * 384

F32 = mybir.dt.float32
BF16 = mybir.dt.bfloat16
I32 = mybir.dt.int32
U8 = mybir.dt.uint8
FP4X4 = mybir.dt.float4_e2m1fn_x4
ALU = mybir.AluOpType
ACTF = mybir.ActivationFunctionType

P = 128
PASSES = 16
D = 128
HALF = 64
ROPE_BASE = 10000.0

ALL8 = 6
SB = 8
TURN = 12
SC = 6
JOINED = 6
VECTOR_ZEROS = 5
XS_FIRST = 3
LATE = 3

TWO_PI = 2.0 * math.pi
C1 = 6.28125
C2 = TWO_PI - C1
WARM_MATMULS = 14


def load_order():
    every = (0, 1, 2, 3)
    order = [("wc", 0, 1, ()), ("xc0", 0, 1, ()), ("ws", 0, ALL8, (0, 1)), ("xsf", 0, XS_FIRST, every), ("ws", 0, ALL8, (2, 3))]
    order += [("xc1", 0, 1, ()), ("xf", 1, 2, ()), ("wc", 1, 2, ()), ("xf", 2, 4, ()), ("wc", 2, 4, ()), ("xsf", XS_FIRST, ALL8, every), ("xf", 4, ALL8, ()), ("wc", 4, ALL8, ())]
    order += [("xs0", ALL8, PASSES, every), ("ws", ALL8, PASSES, every)]
    for g in range(ALL8, PASSES, 2):
        order += [("xc0", g, g + 2, ()), ("wc", g, g + 2, ())]
    order += [("xs1", ALL8, PASSES, every)]
    for g in range(ALL8, PASSES, 2):
        order += [("xc1", g, g + 2, ())]
    return order


def tile_attentionhead_pa_kernel(tc, x_words, x_scales, W_qkv_words, W_qkv_scales, sqk, out_0, out_1, out_2):
    nc = tc.nc
    q_out = out_0.rearrange("b t d -> (b t) d")
    k_out = out_1.rearrange("b t d -> (b t) d")
    v_out = out_2.rearrange("b t d -> (b t) d")

    with ExitStack() as ctx:
        keep = ctx.enter_context(tc.tile_pool(name="keep", bufs=1))
        work = ctx.enter_context(tc.tile_pool(name="work", bufs=4))
        psum = ctx.enter_context(tc.psum_pool(name="psum", bufs=1))
        ctx.enter_context(tc.manual_schedule())

        widths = {"xf": 2048, "xc0": 1024, "xc1": 1024, "wc": 1024, "xsf": 1024, "xs0": 512, "xs1": 512, "ws": 512}
        where = {}
        loads = []
        planes = []
        for kind, g0, g1, rows in load_order():
            if (kind, g0) in where:
                t = where[(kind, g0)][0]
            else:
                t = keep.tile([P, g1 - g0, widths[kind]], U8, name="%s_%d" % (kind, g0), align_bytes=256)
                if len(rows) > 0:
                    planes.append(t)
            loads.append((kind, g0, g1, rows, t))
            for g in range(g0, g1):
                where[(kind, g)] = (t, g - g0)

        zero1 = keep.tile([P, 1], F32, name="zero1")
        junk1 = keep.tile([P, 1], F32, name="junk1")
        g_row = keep.tile([P, D], BF16, name="g_row")
        ones = keep.tile([P, 512], BF16, name="ones")
        gain = keep.tile([P, D], F32, name="gain")
        pos_i = keep.tile([P, 4], I32, name="pos_i")
        pos_f = keep.tile([P, 4], F32, name="pos_f")
        freq = keep.tile([P, HALF], F32, name="freq")
        ang = keep.tile([P, 256], F32, name="ang")
        turns = keep.tile([P, 256], I32, name="turns")
        red1 = keep.tile([P, 256], F32, name="red1")
        red = keep.tile([P, 256], F32, name="red")
        s2 = keep.tile([P, 256], F32, name="s2")
        s4 = keep.tile([P, 256], F32, name="s4")
        q2 = keep.tile([P, 256], F32, name="q2")
        q4 = keep.tile([P, 256], F32, name="q4")
        c2 = keep.tile([P, 256], F32, name="c2")
        cos1 = keep.tile([P, 256], F32, name="cos1")
        sin1 = keep.tile([P, 256], F32, name="sin1")
        cos_t = keep.tile([P, 1024], F32, name="cos_t")
        sin_t = keep.tile([P, 1024], F32, name="sin_t")

        v_early = {}
        for i in range(4, JOINED):
            v_early[i] = keep.tile([P, D], F32, name="v_early%d" % i)

        nc.vector.memset(ones[:], 1.0)
        for t in planes[:VECTOR_ZEROS]:
            nc.vector.memset(t[:].bitcast(I32), 0)
        nc.vector.memset(zero1[:], 0.0)
        nc.vector.memset(g_row[:], 0.0)
        nc.gpsimd.dma_start(out=g_row[0:1, :], in_=sqk.rearrange("(o d) -> o d", o=1))
        nc.gpsimd.iota(pos_i[:], pattern=[[P, 4]], base=0, channel_multiplier=1)
        for t in planes[VECTOR_ZEROS:]:
            nc.gpsimd.memset(t[:].bitcast(F32), 0.0)

        for kind, a, b, rows, t in loads:
            if len(rows) > 0:
                for r in rows:
                    if kind == "xsf":
                        src = x_scales[a:b, r:16:4, :]
                    elif kind == "xs0":
                        src = x_scales[a:b, r:16:4, 0:512]
                    elif kind == "xs1":
                        src = x_scales[a:b, r:16:4, 512:1024]
                    else:
                        src = W_qkv_scales[a:b, r:16:4, :]
                    wide = 384 if kind == "ws" else widths[kind]
                    nc.sync.dma_start(out=t[r:P:32, :, 0:wide].bitcast(I32), in_=src.rearrange("g q c -> q g c").bitcast(I32))
            else:
                if kind == "xf":
                    src = x_words[a:b, :, :]
                elif kind == "xc0":
                    src = x_words[a:b, :, 0:1024]
                elif kind == "xc1":
                    src = x_words[a:b, :, 1024:2048]
                else:
                    src = W_qkv_words[a:b, :, :]
                wide = 768 if kind == "wc" else widths[kind]
                nc.sync.dma_start(out=t[:, :, 0:wide].bitcast(I32), in_=src.rearrange("g p b -> p g b").bitcast(I32))

        nc.scalar.activation(out=junk1[:], in_=zero1[:], func=ACTF.Sin)
        g_ps = psum.tile([P, 512], F32, name="bank7")
        for n in range(WARM_MATMULS):
            nc.tensor.matmul(out=g_ps[:], lhsT=ones[:, 0:P], rhs=ones[:], start=True, stop=True)
        def mm(bank, part, i, g, o0, first, last):
            if ("xf", g) in where:
                xt, xl = where[("xf", g)]
                cl = i
            else:
                xt, xl = where[("xc%d" % (i // 4), g)]
                cl = i % 4
            if g < ALL8:
                st, sl = where[("xsf", g)]
                il = i
            else:
                st, sl = where[("xs%d" % (i // 4), g)]
                il = i % 4
            wt, wl = where[("wc", g)]
            pt, pl = where[("ws", g)]
            if part == "qk":
                c0, c1 = 0, 256
            else:
                c0, c1 = 256, 384
            nc.tensor.matmul_mx(
                out=bank[:, o0 : o0 + c1 - c0],
                lhsT=xt[:, xl, 256 * cl : 256 * (cl + 1)].bitcast(FP4X4),
                lhsT_scale=st[:, sl, P * il : P * (il + 1)],
                rhs=wt[:, wl, 2 * c0 : 2 * c1].bitcast(FP4X4),
                rhs_scale=pt[:, pl, c0:c1],
                start=first,
                stop=last,
            )

        def qk(i, g):
            mm(bank[i], "qk", i, g, 0, g == (LATE if i == 7 else 0), (i >= 4 or i % 2 == 1) and g == PASSES - 1)

        def v_joined(i, g):
            mm(bank[i], "v", i, g, 256, False, False)

        def v_turned(j, g):
            if ("xf", g) in where:
                xt, xl = where[("xf", g)]
            else:
                xt, xl = where[("xc0", g)]
            if g < ALL8:
                st, sl = where[("xsf", g)]
            else:
                st, sl = where[("xs0", g)]
            wt, wl = where[("wc", g)]
            pt, pl = where[("ws", g)]
            nc.tensor.matmul_mx(
                out=bank[2 * j][:, 256:512],
                lhsT=wt[:, wl, 512:768].bitcast(FP4X4),
                lhsT_scale=pt[:, pl, 256:384],
                rhs=xt[:, xl, 512 * j : 512 * (j + 1)].bitcast(FP4X4),
                rhs_scale=st[:, sl, 256 * j : 256 * (j + 1)],
                start=False,
                stop=(g == PASSES - 1),
            )

        def step(i, g):
            qk(i, g)
            if i < 4:
                if i % 2 == 0:
                    v_turned(i // 2, g)
            elif i < JOINED and g < ALL8:
                v_joined(i, g)

        state = {}
        recip = {}

        def norms(i):
            sq = work.tile([P, D], F32, name="sq")
            ss = work.tile([P, 2], F32, name="ss")
            nc.scalar.activation(out=sq[:], in_=bank[i][:, 0:D], func=ACTF.Square, accum_out=ss[:, 0:1])
            sq_k = work.tile([P, D], F32, name="sq")
            nc.scalar.activation(out=sq_k[:], in_=bank[i][:, D : 2 * D], func=ACTF.Square, accum_out=ss[:, 1:2])
            rn = work.tile([P, 2], F32, name="rn")
            nc.scalar.activation(out=rn[:], in_=ss[:], func=ACTF.Abs_reciprocal_sqrt)
            recip[i] = rn

        def rope_products(i):
            t = i % 4
            t1 = work.tile([P, 256], F32, name="t1")
            nc.vector.tensor_tensor(out=t1[:], in0=bank[i][:, 0:256], in1=cos_t[:, 256 * t : 256 * (t + 1)], op=ALU.mult)
            t2 = work.tile([P, 256], F32, name="t2")
            raw_v = bank[i][:, 0:256].rearrange("p (a h j) -> p a h j", a=2, h=2)
            t2_v = t2[:].rearrange("p (a h j) -> p a h j", a=2, h=2)
            nc.vector.tensor_tensor(out=t2_v[:, :, :, :], in0=raw_v[:, :, ::-1, :], in1=sin_v[:, t, :, :, :], op=ALU.mult)
            state[i] = [t1, t2]

        def rope_add(i):
            t1, t2 = state[i]
            sm = work.tile([P, 256], F32, name="sm")
            nc.vector.tensor_tensor(out=sm[:], in0=t1[:], in1=t2[:], op=ALU.add)
            state[i] = sm

        def v_copy(i):
            if i < 4:
                if i % 2 == 0:
                    turned = work.tile([P, 256], F32, name="turned", align_bytes=64)
                    nc.vector.transpose(out=turned[:, 0:128], in_=bank[i][:, 256:384])
                    nc.vector.transpose(out=turned[:, 128:256], in_=bank[i][:, 384:512])
                    for c in range(4):
                        nc.sync.dma_start(
                            out=v_out[P * i : P * (i + 2), 32 * c : 32 * (c + 1)].rearrange("(n a) b -> a n b", a=32),
                            in_=turned[32 * c : 32 * (c + 1), :].rearrange("p (n b) -> p n b", b=32),
                        )
            elif i < JOINED:
                nc.scalar.copy(out=v_early[i][:], in_=bank[i][:, 256:384])

        def scale_store(i):
            sm = state[i]
            rn = recip[i]
            res = work.tile([P, 256], F32, name="res")
            nc.scalar.activation(out=res[:, 0:D], in_=sm[:, 0:D], func=ACTF.Copy, scale=rn[:, 0:1])
            nc.scalar.activation(out=res[:, D : 2 * D], in_=sm[:, D : 2 * D], func=ACTF.Copy, scale=rn[:, 1:2])
            nc.sync.dma_start(out=q_out[P * i : P * (i + 1), :], in_=res[:, 0:D])
            nc.sync.dma_start(out=k_out[P * i : P * (i + 1), :], in_=res[:, D : 2 * D])

        bank = {}
        for i in range(7):
            bank[i] = psum.tile([P, 512], F32, name="bank%d" % i)

        for g in range(LATE):
            for i in range(7):
                step(i, g)

        nc.tensor.matmul(out=g_ps[:, 0:D], lhsT=ones[:, 0:P], rhs=g_row[:], start=True, stop=True)
        nc.scalar.copy(out=gain[:], in_=g_ps[:, 0:D])

        nc.vector.memset(freq[:, 0:1], 1.0)
        w = 1
        while w < HALF:
            nc.vector.tensor_scalar(out=freq[:, w : 2 * w], in0=freq[:, 0:w], scalar1=ROPE_BASE ** (-w / 64.0), scalar2=None, op0=ALU.mult)
            w *= 2
        nc.vector.tensor_copy(out=pos_f[:], in_=pos_i[:])
        for t in range(4):
            nc.vector.tensor_scalar(out=ang[:, HALF * t : HALF * (t + 1)], in0=freq[:], scalar1=pos_f[:, t : t + 1], scalar2=None, op0=ALU.mult)
        nc.vector.tensor_scalar(out=turns[:], in0=ang[:], scalar1=1.0 / TWO_PI, scalar2=0.25, op0=ALU.mult, op1=ALU.add)
        nc.vector.scalar_tensor_tensor(out=red1[:], in0=turns[:], scalar=-C1, in1=ang[:], op0=ALU.mult, op1=ALU.add)
        nc.vector.scalar_tensor_tensor(out=red[:], in0=turns[:], scalar=-C2, in1=red1[:], op0=ALU.mult, op1=ALU.add)
        nc.scalar.activation(out=s4[:], in_=red[:], func=ACTF.Sin, scale=0.25)
        nc.scalar.activation(out=s2[:], in_=red[:], func=ACTF.Sin, scale=0.5)
        nc.scalar.activation(out=q4[:], in_=s4[:], func=ACTF.Square)
        nc.scalar.activation(out=q2[:], in_=s2[:], func=ACTF.Square)
        nc.vector.tensor_scalar(out=c2[:], in0=q4[:], scalar1=-2.0, scalar2=1.0, op0=ALU.mult, op1=ALU.add)
        cos_v = cos_t[:].rearrange("p (t a h j) -> p t a h j", t=4, a=2, h=2)
        sin_v = sin_t[:].rearrange("p (t a h j) -> p t a h j", t=4, a=2, h=2)
        nc.scalar.activation(out=junk1[:], in_=freq[:, 0:1], func=ACTF.Abs_reciprocal_sqrt)
        nc.vector.tensor_scalar(out=cos1[:], in0=q2[:], scalar1=-2.0, scalar2=1.0, op0=ALU.mult, op1=ALU.add)
        nc.vector.scalar_tensor_tensor(out=sin1[:], in0=s2[:], scalar=2.0, in1=c2[:], op0=ALU.mult, op1=ALU.mult)
        for t in range(4):
            for h in range(2):
                nc.vector.tensor_tensor(out=cos_v[:, t, 0, h, :], in0=cos1[:, HALF * t : HALF * (t + 1)], in1=gain[:, HALF * h : HALF * (h + 1)], op=ALU.mult)
                nc.vector.scalar_tensor_tensor(out=sin_v[:, t, 0, h, :], in0=sin1[:, HALF * t : HALF * (t + 1)], scalar=(-1.0 if h == 0 else 1.0), in1=gain[:, HALF * h : HALF * (h + 1)], op0=ALU.mult, op1=ALU.mult)
        nc.vector.tensor_copy(out=cos_v[:, :, 1, :, :], in_=cos_v[:, :, 0, :, :])
        nc.vector.tensor_copy(out=sin_v[:, :, 1, :, :], in_=sin_v[:, :, 0, :, :])


        bank[7] = psum.tile([P, 512], F32, name="bank7")
        for g in range(LATE, ALL8):
            for i in range(8):
                step(i, g)
        for g in range(LATE):
            step(7, g)
        for g in range(ALL8, SB):
            for i in range(4):
                step(i, g)
        for g0, g1 in ((SB, TURN), (TURN, PASSES)):
            for i in range(2):
                for g in range(g0, g1):
                    step(i, g)
        for i in range(2, 4):
            for g in range(SB, PASSES):
                step(i, g)
        for g in range(ALL8, SC):
            for i in range(4, 8):
                qk(i, g)
        for i in range(4, 8):
            for g in range(SC, PASSES):
                qk(i, g)

        for i in range(8):
            rope_products(i)
            norms(i)
            if i > 0:
                rope_add(i - 1)
                v_copy(i - 1)
                scale_store(i - 1)
        rope_add(7)
        v_copy(7)
        scale_store(7)

        for i in range(4, 8):
            late = psum.tile([P, 512], F32, name="bank%d" % (i - 4))
            g0 = ALL8 if i < JOINED else 0
            for g in range(g0, PASSES):
                mm(late, "v", i, g, 0, g == g0, g == PASSES - 1)
            vt = work.tile([P, D], F32, name="vt")
            if i < JOINED:
                nc.vector.tensor_tensor(out=vt[:], in0=late[:, 0:D], in1=v_early[i][:], op=ALU.add)
            else:
                nc.scalar.copy(out=vt[:], in_=late[:, 0:D])
            nc.sync.dma_start(out=v_out[P * i : P * (i + 1), :], in_=vt[:])
